import numpy as np
import ml_dtypes


def mxq(x, axis, fmt="e4m3"):
    dtype, down = {"e4m3": (ml_dtypes.float8_e4m3fn, 7), "e5m2": (ml_dtypes.float8_e5m2, 14)}[fmt]
    v = np.moveaxis(np.asarray(x, np.float32).astype(ml_dtypes.bfloat16).astype(np.float64), axis, -1)
    blocks = v.reshape(v.shape[:-1] + (-1, 32))
    amax = np.abs(blocks).max(-1, keepdims=True)
    byte = np.maximum(np.where(amax > 0, np.frexp(amax)[1] - 1 + 127, 0) - down, 1)
    scale = np.exp2(byte - 127.0)
    codes = (blocks / scale).astype(np.float32).astype(dtype).astype(np.float64)
    return np.moveaxis((codes * scale).reshape(v.shape), -1, axis)


WIDE = False


def mx_kscale(k):
    if not WIDE:
        return np.ones(k)
    levels = np.array([10, -10, 5, -5, 0])
    a = np.random.permutation(np.resize(levels, k // 512 * 4)).reshape(k // 512, 4)
    idx = np.arange(k)
    return np.exp2(a[idx // 512, idx % 128 // 32])


BF16 = ml_dtypes.bfloat16


def bf(x):
    return np.asarray(x, np.float32).astype(BF16)


def f64(x):
    return np.asarray(x).astype(np.float64)


B, N, D, H = 16, 512, 128, 512
EDGE_P = 0.01
DEG = 1.0 + EDGE_P * N


def normalize_adj(adj):
    rowsum = adj.sum(axis=1)
    d_inv_sqrt = np.where(rowsum > 0, 1.0 / np.sqrt(np.maximum(rowsum, 1e-30)), 0.0)
    return d_inv_sqrt[:, :, None] * adj.transpose(0, 2, 1) * d_inv_sqrt[:, None, :]


def setup_inputs():
    t = mx_kscale(H)
    adj = (np.random.uniform(size=(B, N, N)) < EDGE_P).astype(np.float64)
    adj = np.minimum(adj + np.eye(N)[None], 1.0)
    return {"msg": bf(np.random.standard_normal((B, N, H)) * 0.5 * np.sqrt(DEG) * t),
            "adj": bf(adj),
            "b2": bf(np.random.standard_normal(H) * 0.2 * t),
            "W3": bf(np.random.standard_normal((H, D)) * 0.5 * np.sqrt(DEG / H) / t[:, None])}


def reference(msg, adj, b2, W3):
    a = normalize_adj(f64(adj))
    h = np.maximum((mxq(a, 2, "e4m3") @ mxq(f64(msg), 1, "e4m3")) + f64(b2), 0.0)
    return mxq(h, 2, "e4m3") @ mxq(f64(W3), 0, "e4m3")

@@ -1,0 +1,249 @@
+import concourse.mybir as mybir
+from concourse.masks import make_identity
+
+F32 = mybir.dt.float32
+BF16 = mybir.dt.bfloat16
+U32 = mybir.dt.uint32
+U8 = mybir.dt.uint8
+FP8X4 = mybir.dt.float8_e4m3fn_x4
+ACT = mybir.ActivationFunctionType
+ALU = mybir.AluOpType
+
+P = 128
+PACK = 4
+GRAPHS = 16
+NODES = 512
+HIDDEN = 512
+OUT = 128
+ONES_COLS = 32
+
+FLOPS = 2 * GRAPHS * (NODES * NODES * HIDDEN + NODES * HIDDEN * OUT)
+
+
+def regroup(nc, grouped, rows):
+    nc.vector.tensor_copy(
+        out=grouped.rearrange("p (c i) t -> p c t i", i=4),
+        in_=rows.rearrange("p t (c i) -> p c t i", i=4),
+    )
+
+
+def quantise(nc, codes, scales, grouped):
+    nc.vector.quantize_mx(
+        out=codes.bitcast(FP8X4),
+        scales=scales,
+        in_=grouped.rearrange("p w t -> p (w t)"),
+    )
+
+
+def tile_perception_pb_t_kernel(tc, msg, adj, b2, W3, out):
+    nc = tc.nc
+    with (
+        tc.tile_pool(name="const", bufs=1) as const,
+        tc.tile_pool(name="inputs", bufs=1) as inputs,
+        tc.tile_pool(name="work", bufs=2) as work,
+        tc.psum_pool(name="psum_deg", bufs=1) as psum_deg,
+        tc.psum_pool(name="psum_bcast", bufs=2) as psum_bcast,
+        tc.psum_pool(name="psum_h", bufs=PACK) as psum_h,
+        tc.psum_pool(name="psum_out", bufs=1) as psum_out,
+        tc.manual_schedule(),
+    ):
+        b2_rows = const.tile([P, P], BF16)
+        nc.vector.memset(b2_rows[:], 0.0)
+        nc.scalar.dma_start(out=b2_rows[0:PACK, :], in_=b2.rearrange("(t p) -> t p", p=P))
+        w3_rows = const.tile([P, PACK, OUT], BF16)
+        nc.scalar.dma_start(out=w3_rows[:], in_=W3.rearrange("(t p) o -> p t o", p=P))
+        adj_rows = []
+        msg_rows = []
+        for g in range(GRAPHS):
+            adj_g = inputs.tile([P, PACK, NODES], BF16, name="adj%d" % g)
+            nc.sync.dma_start(out=adj_g[:], in_=adj[g].rearrange("(t p) i -> p t i", p=P))
+            adj_rows.append(adj_g)
+            msg_g = inputs.tile([P, PACK, HIDDEN], BF16, name="msg%d" % g)
+            nc.sync.dma_start(out=msg_g[:], in_=msg[g].rearrange("(t p) f -> p t f", p=P))
+            msg_rows.append(msg_g)
+
+        ident = const.tile([P, P], F32)
+        make_identity(nc, ident[:])
+        ones = const.tile([P, ONES_COLS], BF16)
+        nc.vector.memset(ones[:], 1.0)
+
+        state = {}
+
+        def degrees(g):
+            deg = psum_deg.tile([P, PACK, ONES_COLS], F32, name="deg")
+            for s in range(PACK):
+                for t in range(PACK):
+                    nc.tensor.matmul(
+                        out=deg[:, s, :],
+                        lhsT=adj_rows[g][:, t, s * P : (s + 1) * P],
+                        rhs=ones[:],
+                        start=(t == 0),
+                        stop=(t == PACK - 1),
+                    )
+            floored = work.tile([P, PACK], F32, name="floored")
+            nc.vector.tensor_scalar_max(out=floored[:], in0=deg[:, :, 0], scalar1=1e-30)
+            state["deg", g] = deg
+            state["floored", g] = floored
+
+        def inverse_root(g):
+            root = work.tile([P, PACK], F32, name="root")
+            nc.scalar.activation(out=root[:], in_=state["floored", g][:], func=ACT.Abs_reciprocal_sqrt)
+            state["root", g] = root
+
+        def spread_d(g):
+            d = work.tile([P, PACK], F32, name="d")
+            nc.vector.scalar_tensor_tensor(
+                out=d[:],
+                in0=state["deg", g][:, :, 0],
+                scalar=0.0,
+                in1=state["root", g][:],
+                op0=ALU.is_gt,
+                op1=ALU.mult,
+            )
+            d_all = psum_bcast.tile([P, NODES], F32, tag="bcast", name="d_all")
+            for t in range(PACK):
+                nc.tensor.transpose(
+                    d_all[:, t * P : (t + 1) * P], d[:, t : t + 1].to_broadcast([P, P]), ident[:]
+                )
+            state["d", g] = d
+            state["d_all", g] = d_all
+
+        def scale_rows(g):
+            half_a = work.tile([P, PACK, NODES], F32, name="half_a")
+            for t in range(PACK):
+                nc.scalar.activation(
+                    out=half_a[:, t, :],
+                    in_=adj_rows[g][:, t, :],
+                    func=ACT.Copy,
+                    scale=state["d", g][:, t : t + 1],
+                )
+            state["half_a", g] = half_a
+
+        def scale_columns(g):
+            a_grouped = work.tile([P, NODES, PACK], BF16, name="a_grouped", align_bytes=64)
+            nc.vector.tensor_tensor(
+                out=a_grouped[:],
+                in0=state["half_a", g][:].rearrange("p t i -> p i t"),
+                in1=state["d_all", g][:].unsqueeze(2).to_broadcast([P, NODES, PACK]),
+                op=ALU.mult,
+            )
+            state["a_grouped", g] = a_grouped
+
+        def regroup_msg(g):
+            msg_grouped = work.tile([P, HIDDEN, PACK], BF16, name="msg_grouped", align_bytes=64)
+            regroup(nc, msg_grouped[:], msg_rows[g][:])
+            state["msg_grouped", g] = msg_grouped
+
+        def quantise_msg(g):
+            msg_codes = work.tile([P, HIDDEN], U32, name="msg_codes", align_bytes=64)
+            msg_scales = work.tile([P, HIDDEN], U8, name="msg_scales", align_bytes=64)
+            quantise(nc, msg_codes[:], msg_scales[:], state["msg_grouped", g][:])
+            state["msg_codes", g] = msg_codes
+            state["msg_scales", g] = msg_scales
+
+        def aggregate(g):
+            a_codes = work.tile([P, NODES], U32, name="a_codes", align_bytes=64)
+            a_scales = work.tile([P, NODES], U8, name="a_scales", align_bytes=64)
+            quantise(nc, a_codes[:], a_scales[:], state["a_grouped", g][:])
+            sums = []
+            for t in range(PACK):
+                f_cols = slice(t * P, (t + 1) * P)
+                sums_t = psum_h.tile([P, NODES], F32, name="sums", tag="sums")
+                nc.tensor.matmul_mx(
+                    out=sums_t[:],
+                    lhsT=state["msg_codes", g][:, f_cols].bitcast(FP8X4),
+                    lhsT_scale=state["msg_scales", g][:, f_cols],
+                    rhs=a_codes[:].bitcast(FP8X4),
+                    rhs_scale=a_scales[:],
+                    start=True,
+                    stop=True,
+                )
+                sums.append(sums_t)
+            state["sums", g] = sums
+
+        def bias_relu(g):
+            h_rows = work.tile([P, PACK, NODES], BF16, name="h_rows")
+            for t in range(PACK):
+                nc.scalar.activation(
+                    out=h_rows[:, t, :],
+                    in_=state["sums", g][t][:],
+                    func=ACT.Relu,
+                    bias=bias[:, t : t + 1],
+                    scale=1.0,
+                )
+            state["h_rows", g] = h_rows
+
+        def regroup_h(g):
+            h_grouped = work.tile([P, NODES, PACK], BF16, name="h_grouped", align_bytes=64)
+            regroup(nc, h_grouped[:], state["h_rows", g][:])
+            state["h_grouped", g] = h_grouped
+
+        def project(g):
+            h_codes = work.tile([P, NODES], U32, name="h_codes", align_bytes=64)
+            h_scales = work.tile([P, NODES], U8, name="h_scales", align_bytes=64)
+            quantise(nc, h_codes[:], h_scales[:], state["h_grouped", g][:])
+            proj = psum_out.tile([P, PACK, OUT], F32, name="proj")
+            for s in range(PACK):
+                i_cols = slice(s * P, (s + 1) * P)
+                nc.tensor.matmul_mx(
+                    out=proj[:, s, :],
+                    lhsT=h_codes[:, i_cols].bitcast(FP8X4),
+                    lhsT_scale=h_scales[:, i_cols],
+                    rhs=w3_codes[:].bitcast(FP8X4),
+                    rhs_scale=w3_scales[:],
+                    start=True,
+                    stop=True,
+                )
+            state["proj", g] = proj
+
+        def store(g):
+            result = work.tile([P, PACK, OUT], F32, name="result")
+            nc.scalar.copy(out=result[:], in_=state["proj", g][:])
+            nc.sync.dma_start(out=out[g].rearrange("(s p) o -> p s o", p=P), in_=result[:])
+
+        degrees(0)
+        inverse_root(0)
+        spread_d(0)
+        scale_rows(0)
+        regroup_msg(0)
+        quantise_msg(0)
+
+        b2_rows_f32 = const.tile([P, P], F32)
+        nc.vector.tensor_copy(out=b2_rows_f32[:], in_=b2_rows[:])
+        b2_cols = psum_bcast.tile([P, NODES], F32, tag="bcast")
+        nc.tensor.transpose(b2_cols[:, 0:P], b2_rows_f32[:], ident[:])
+        bias = const.tile([P, PACK], F32)
+        nc.vector.tensor_copy(out=bias[:], in_=b2_cols[:, 0:PACK])
+
+        w3_grouped = const.tile([P, OUT, PACK], BF16, align_bytes=64)
+        regroup(nc, w3_grouped[:], w3_rows[:])
+        w3_codes = const.tile([P, OUT], U32, align_bytes=64)
+        w3_scales = const.tile([P, OUT], U8, align_bytes=64)
+        quantise(nc, w3_codes[:], w3_scales[:], w3_grouped[:])
+
+        def live(g):
+            return 0 <= g < GRAPHS
+
+        for k in range(GRAPHS + 2):
+            if live(k + 1):
+                degrees(k + 1)
+            if live(k - 1):
+                bias_relu(k - 1)
+            if live(k + 1):
+                inverse_root(k + 1)
+            if live(k - 2):
+                store(k - 2)
+            if live(k):
+                scale_columns(k)
+            if live(k + 1):
+                spread_d(k + 1)
+                scale_rows(k + 1)
+                regroup_msg(k + 1)
+            if live(k):
+                aggregate(k)
+            if live(k - 1):
+                regroup_h(k - 1)
+            if live(k + 1):
+                quantise_msg(k + 1)
+            if live(k - 1):
+                project(k - 1)

@@ -41,8 +41,8 @@ def tile_perception_pb_t_kernel(tc, msg, adj, b2, W3, out):
         tc.tile_pool(name="const", bufs=1) as const,
         tc.tile_pool(name="inputs", bufs=1) as inputs,
         tc.tile_pool(name="work", bufs=2) as work,
-        tc.psum_pool(name="psum_deg", bufs=1) as psum_deg,
-        tc.psum_pool(name="psum_bcast", bufs=2) as psum_bcast,
+        tc.psum_pool(name="psum_deg", bufs=2) as psum_deg,
+        tc.psum_pool(name="psum_bcast", bufs=1) as psum_bcast,
         tc.psum_pool(name="psum_h", bufs=PACK) as psum_h,
         tc.psum_pool(name="psum_out", bufs=1) as psum_out,
         tc.manual_schedule(),
@@ -54,13 +54,22 @@ def tile_perception_pb_t_kernel(tc, msg, adj, b2, W3, out):
         nc.scalar.dma_start(out=w3_rows[:], in_=W3.rearrange("(t p) o -> p t o", p=P))
         adj_rows = []
         msg_rows = []
-        for g in range(GRAPHS):
+
+        def load_adj(g):
             adj_g = inputs.tile([P, PACK, NODES], BF16, name="adj%d" % g)
             nc.sync.dma_start(out=adj_g[:], in_=adj[g].rearrange("(t p) i -> p t i", p=P))
             adj_rows.append(adj_g)
+
+        def load_msg(g):
             msg_g = inputs.tile([P, PACK, HIDDEN], BF16, name="msg%d" % g)
             nc.sync.dma_start(out=msg_g[:], in_=msg[g].rearrange("(t p) f -> p t f", p=P))
             msg_rows.append(msg_g)
+
+        load_adj(0)
+        for g in range(GRAPHS):
+            if g + 1 < GRAPHS:
+                load_adj(g + 1)
+            load_msg(g)
 
         ident = const.tile([P, P], F32)
         make_identity(nc, ident[:])
@@ -80,9 +89,11 @@ def tile_perception_pb_t_kernel(tc, msg, adj, b2, W3, out):
                         start=(t == 0),
                         stop=(t == PACK - 1),
                     )
-            floored = work.tile([P, PACK], F32, name="floored")
-            nc.vector.tensor_scalar_max(out=floored[:], in0=deg[:, :, 0], scalar1=1e-30)
             state["deg", g] = deg
+
+        def floor_degrees(g):
+            floored = work.tile([P, PACK], F32, name="floored")
+            nc.vector.tensor_scalar_max(out=floored[:], in0=state["deg", g][:, :, 0], scalar1=1e-30)
             state["floored", g] = floored
 
         def inverse_root(g):
@@ -100,7 +111,7 @@ def tile_perception_pb_t_kernel(tc, msg, adj, b2, W3, out):
                 op0=ALU.is_gt,
                 op1=ALU.mult,
             )
-            d_all = psum_bcast.tile([P, NODES], F32, tag="bcast", name="d_all")
+            d_all = psum_bcast.tile([P, NODES], F32, name="d_all")
             for t in range(PACK):
                 nc.tensor.transpose(
                     d_all[:, t * P : (t + 1) * P], d[:, t : t + 1].to_broadcast([P, P]), ident[:]
@@ -182,7 +193,7 @@ def tile_perception_pb_t_kernel(tc, msg, adj, b2, W3, out):
             h_codes = work.tile([P, NODES], U32, name="h_codes", align_bytes=64)
             h_scales = work.tile([P, NODES], U8, name="h_scales", align_bytes=64)
             quantise(nc, h_codes[:], h_scales[:], state["h_grouped", g][:])
-            proj = psum_out.tile([P, PACK, OUT], F32, name="proj")
+            proj = psum_out.tile([P, PACK, OUT], F32, name="proj", tag="proj")
             for s in range(PACK):
                 i_cols = slice(s * P, (s + 1) * P)
                 nc.tensor.matmul_mx(
@@ -201,36 +212,14 @@ def tile_perception_pb_t_kernel(tc, msg, adj, b2, W3, out):
             nc.scalar.copy(out=result[:], in_=state["proj", g][:])
             nc.sync.dma_start(out=out[g].rearrange("(s p) o -> p s o", p=P), in_=result[:])
 
-        degrees(0)
-        inverse_root(0)
-        spread_d(0)
-        scale_rows(0)
-        regroup_msg(0)
-        quantise_msg(0)
-
-        b2_rows_f32 = const.tile([P, P], F32)
-        nc.vector.tensor_copy(out=b2_rows_f32[:], in_=b2_rows[:])
-        b2_cols = psum_bcast.tile([P, NODES], F32, tag="bcast")
-        nc.tensor.transpose(b2_cols[:, 0:P], b2_rows_f32[:], ident[:])
-        bias = const.tile([P, PACK], F32)
-        nc.vector.tensor_copy(out=bias[:], in_=b2_cols[:, 0:PACK])
-
-        w3_grouped = const.tile([P, OUT, PACK], BF16, align_bytes=64)
-        regroup(nc, w3_grouped[:], w3_rows[:])
-        w3_codes = const.tile([P, OUT], U32, align_bytes=64)
-        w3_scales = const.tile([P, OUT], U8, align_bytes=64)
-        quantise(nc, w3_codes[:], w3_scales[:], w3_grouped[:])
-
         def live(g):
             return 0 <= g < GRAPHS
 
-        for k in range(GRAPHS + 2):
-            if live(k + 1):
-                degrees(k + 1)
+        def step(k):
+            if live(k + 2):
+                degrees(k + 2)
             if live(k - 1):
                 bias_relu(k - 1)
-            if live(k + 1):
-                inverse_root(k + 1)
             if live(k - 2):
                 store(k - 2)
             if live(k):
@@ -241,9 +230,31 @@ def tile_perception_pb_t_kernel(tc, msg, adj, b2, W3, out):
                 regroup_msg(k + 1)
             if live(k):
                 aggregate(k)
+            if live(k + 2):
+                floor_degrees(k + 2)
+                inverse_root(k + 2)
             if live(k - 1):
                 regroup_h(k - 1)
             if live(k + 1):
                 quantise_msg(k + 1)
             if live(k - 1):
                 project(k - 1)
+
+        step(-2)
+        step(-1)
+
+        b2_rows_f32 = const.tile([P, P], F32)
+        nc.vector.tensor_copy(out=b2_rows_f32[:], in_=b2_rows[:])
+        b2_cols = psum_out.tile([P, PACK, OUT], F32, tag="proj")
+        nc.tensor.transpose(b2_cols[:, 0, :], b2_rows_f32[:], ident[:])
+        bias = const.tile([P, PACK], F32)
+        nc.vector.tensor_copy(out=bias[:], in_=b2_cols[:, 0, 0:PACK])
+
+        w3_grouped = const.tile([P, OUT, PACK], BF16, align_bytes=64)
+        regroup(nc, w3_grouped[:], w3_rows[:])
+        w3_codes = const.tile([P, OUT], U32, align_bytes=64)
+        w3_scales = const.tile([P, OUT], U8, align_bytes=64)
+        quantise(nc, w3_codes[:], w3_scales[:], w3_grouped[:])
+
+        for k in range(GRAPHS + 2):
+            step(k)

@@ -20,8 +20,8 @@ ONES_COLS = 32
 FLOPS = 2 * GRAPHS * (NODES * NODES * HIDDEN + NODES * HIDDEN * OUT)
 
 
-def regroup(nc, grouped, rows):
-    nc.vector.tensor_copy(
+def regroup(copy, grouped, rows):
+    copy(
         out=grouped.rearrange("p (c i) t -> p c t i", i=4),
         in_=rows.rearrange("p t (c i) -> p c t i", i=4),
     )
@@ -41,8 +41,8 @@ def tile_perception_pb_t_kernel(tc, msg, adj, b2, W3, out):
         tc.tile_pool(name="const", bufs=1) as const,
         tc.tile_pool(name="inputs", bufs=1) as inputs,
         tc.tile_pool(name="work", bufs=2) as work,
-        tc.psum_pool(name="psum_deg", bufs=2) as psum_deg,
-        tc.psum_pool(name="psum_bcast", bufs=1) as psum_bcast,
+        tc.psum_pool(name="psum_deg", bufs=1) as psum_deg,
+        tc.psum_pool(name="psum_bcast", bufs=2) as psum_bcast,
         tc.psum_pool(name="psum_h", bufs=PACK) as psum_h,
         tc.psum_pool(name="psum_out", bufs=1) as psum_out,
         tc.manual_schedule(),
@@ -65,10 +65,8 @@ def tile_perception_pb_t_kernel(tc, msg, adj, b2, W3, out):
             nc.sync.dma_start(out=msg_g[:], in_=msg[g].rearrange("(t p) f -> p t f", p=P))
             msg_rows.append(msg_g)
 
-        load_adj(0)
         for g in range(GRAPHS):
-            if g + 1 < GRAPHS:
-                load_adj(g + 1)
+            load_adj(g)
             load_msg(g)
 
         ident = const.tile([P, P], F32)
@@ -122,11 +120,13 @@ def tile_perception_pb_t_kernel(tc, msg, adj, b2, W3, out):
         def scale_rows(g):
             half_a = work.tile([P, PACK, NODES], F32, name="half_a")
             for t in range(PACK):
-                nc.scalar.activation(
+                nc.gpsimd.tensor_scalar(
                     out=half_a[:, t, :],
-                    in_=adj_rows[g][:, t, :],
-                    func=ACT.Copy,
-                    scale=state["d", g][:, t : t + 1],
+                    in0=adj_rows[g][:, t, :],
+                    scalar1=state["d", g][:, t : t + 1],
+                    scalar2=0.0,
+                    op0=ALU.mult,
+                    op1=ALU.add,
                 )
             state["half_a", g] = half_a
 
@@ -142,7 +142,7 @@ def tile_perception_pb_t_kernel(tc, msg, adj, b2, W3, out):
 
         def regroup_msg(g):
             msg_grouped = work.tile([P, HIDDEN, PACK], BF16, name="msg_grouped", align_bytes=64)
-            regroup(nc, msg_grouped[:], msg_rows[g][:])
+            regroup(nc.scalar.copy, msg_grouped[:], msg_rows[g][:])
             state["msg_grouped", g] = msg_grouped
 
         def quantise_msg(g):
@@ -186,7 +186,7 @@ def tile_perception_pb_t_kernel(tc, msg, adj, b2, W3, out):
 
         def regroup_h(g):
             h_grouped = work.tile([P, NODES, PACK], BF16, name="h_grouped", align_bytes=64)
-            regroup(nc, h_grouped[:], state["h_rows", g][:])
+            regroup(nc.vector.tensor_copy, h_grouped[:], state["h_rows", g][:])
             state["h_grouped", g] = h_grouped
 
         def project(g):
@@ -216,29 +216,31 @@ def tile_perception_pb_t_kernel(tc, msg, adj, b2, W3, out):
             return 0 <= g < GRAPHS
 
         def step(k):
+            if live(k):
+                scale_columns(k)
+            if live(k + 1):
+                scale_rows(k + 1)
             if live(k + 2):
                 degrees(k + 2)
             if live(k - 1):
                 bias_relu(k - 1)
-            if live(k - 2):
-                store(k - 2)
-            if live(k):
-                scale_columns(k)
-            if live(k + 1):
-                spread_d(k + 1)
-                scale_rows(k + 1)
-                regroup_msg(k + 1)
-            if live(k):
-                aggregate(k)
             if live(k + 2):
                 floor_degrees(k + 2)
                 inverse_root(k + 2)
-            if live(k - 1):
-                regroup_h(k - 1)
+            if live(k - 2):
+                project(k - 2)
             if live(k + 1):
                 quantise_msg(k + 1)
+            if live(k):
+                aggregate(k)
+            if live(k + 2):
+                regroup_msg(k + 2)
+            if live(k - 2):
+                store(k - 2)
             if live(k - 1):
-                project(k - 1)
+                regroup_h(k - 1)
+            if live(k + 2):
+                spread_d(k + 2)
 
         step(-2)
         step(-1)
@@ -251,7 +253,7 @@ def tile_perception_pb_t_kernel(tc, msg, adj, b2, W3, out):
         nc.vector.tensor_copy(out=bias[:], in_=b2_cols[:, 0, 0:PACK])
 
         w3_grouped = const.tile([P, OUT, PACK], BF16, align_bytes=64)
-        regroup(nc, w3_grouped[:], w3_rows[:])
+        regroup(nc.vector.tensor_copy, w3_grouped[:], w3_rows[:])
         w3_codes = const.tile([P, OUT], U32, align_bytes=64)
         w3_scales = const.tile([P, OUT], U8, align_bytes=64)
         quantise(nc, w3_codes[:], w3_scales[:], w3_grouped[:])

@@ -133,9 +133,12 @@ def tile_perception_pb_t_kernel(tc, msg, adj, b2, W3, out):
         def scale_columns(g):
             a_grouped = work.tile([P, NODES, PACK], BF16, name="a_grouped", align_bytes=64)
             nc.vector.tensor_tensor(
-                out=a_grouped[:],
-                in0=state["half_a", g][:].rearrange("p t i -> p i t"),
-                in1=state["d_all", g][:].unsqueeze(2).to_broadcast([P, NODES, PACK]),
+                out=a_grouped[:].rearrange("p (c i) t -> p c t i", i=4),
+                in0=state["half_a", g][:].rearrange("p t (c i) -> p c t i", i=4),
+                in1=state["d_all", g][:]
+                .rearrange("p (c i) -> p c i", i=4)
+                .unsqueeze(2)
+                .to_broadcast([P, NODES // 4, PACK, 4]),
                 op=ALU.mult,
             )
             state["a_grouped", g] = a_grouped

@@ -11,6 +11,7 @@ ALU = mybir.AluOpType
 
 P = 128
 PACK = 4
+RUN = 4
 GRAPHS = 16
 NODES = 512
 HIDDEN = 512
@@ -20,11 +21,16 @@ ONES_COLS = 32
 FLOPS = 2 * GRAPHS * (NODES * NODES * HIDDEN + NODES * HIDDEN * OUT)
 
 
+def by_runs_grouped(grouped):
+    return grouped.rearrange("p (c i) t -> p c t i", i=RUN)
+
+
+def by_runs_rows(rows):
+    return rows.rearrange("p t (c i) -> p c t i", i=RUN)
+
+
 def regroup(copy, grouped, rows):
-    copy(
-        out=grouped.rearrange("p (c i) t -> p c t i", i=4),
-        in_=rows.rearrange("p t (c i) -> p c t i", i=4),
-    )
+    copy(out=by_runs_grouped(grouped), in_=by_runs_rows(rows))
 
 
 def quantise(nc, codes, scales, grouped):
@@ -41,8 +47,9 @@ def tile_perception_pb_t_kernel(tc, msg, adj, b2, W3, out):
         tc.tile_pool(name="const", bufs=1) as const,
         tc.tile_pool(name="inputs", bufs=1) as inputs,
         tc.tile_pool(name="work", bufs=2) as work,
-        tc.psum_pool(name="psum_deg", bufs=1) as psum_deg,
-        tc.psum_pool(name="psum_bcast", bufs=2) as psum_bcast,
+        tc.tile_pool(name="ahead", bufs=3) as ahead,
+        tc.psum_pool(name="psum_deg", bufs=2) as psum_deg,
+        tc.psum_pool(name="psum_bcast", bufs=1) as psum_bcast,
         tc.psum_pool(name="psum_h", bufs=PACK) as psum_h,
         tc.psum_pool(name="psum_out", bufs=1) as psum_out,
         tc.manual_schedule(),
@@ -65,188 +72,16 @@ def tile_perception_pb_t_kernel(tc, msg, adj, b2, W3, out):
             nc.sync.dma_start(out=msg_g[:], in_=msg[g].rearrange("(t p) f -> p t f", p=P))
             msg_rows.append(msg_g)
 
+        load_adj(0)
         for g in range(GRAPHS):
-            load_adj(g)
+            if g + 1 < GRAPHS:
+                load_adj(g + 1)
             load_msg(g)
 
         ident = const.tile([P, P], F32)
         make_identity(nc, ident[:])
         ones = const.tile([P, ONES_COLS], BF16)
         nc.vector.memset(ones[:], 1.0)
-
-        state = {}
-
-        def degrees(g):
-            deg = psum_deg.tile([P, PACK, ONES_COLS], F32, name="deg")
-            for s in range(PACK):
-                for t in range(PACK):
-                    nc.tensor.matmul(
-                        out=deg[:, s, :],
-                        lhsT=adj_rows[g][:, t, s * P : (s + 1) * P],
-                        rhs=ones[:],
-                        start=(t == 0),
-                        stop=(t == PACK - 1),
-                    )
-            state["deg", g] = deg
-
-        def floor_degrees(g):
-            floored = work.tile([P, PACK], F32, name="floored")
-            nc.vector.tensor_scalar_max(out=floored[:], in0=state["deg", g][:, :, 0], scalar1=1e-30)
-            state["floored", g] = floored
-
-        def inverse_root(g):
-            root = work.tile([P, PACK], F32, name="root")
-            nc.scalar.activation(out=root[:], in_=state["floored", g][:], func=ACT.Abs_reciprocal_sqrt)
-            state["root", g] = root
-
-        def spread_d(g):
-            d = work.tile([P, PACK], F32, name="d")
-            nc.vector.scalar_tensor_tensor(
-                out=d[:],
-                in0=state["deg", g][:, :, 0],
-                scalar=0.0,
-                in1=state["root", g][:],
-                op0=ALU.is_gt,
-                op1=ALU.mult,
-            )
-            d_all = psum_bcast.tile([P, NODES], F32, name="d_all")
-            for t in range(PACK):
-                nc.tensor.transpose(
-                    d_all[:, t * P : (t + 1) * P], d[:, t : t + 1].to_broadcast([P, P]), ident[:]
-                )
-            state["d", g] = d
-            state["d_all", g] = d_all
-
-        def scale_rows(g):
-            half_a = work.tile([P, PACK, NODES], F32, name="half_a")
-            for t in range(PACK):
-                nc.gpsimd.tensor_scalar(
-                    out=half_a[:, t, :],
-                    in0=adj_rows[g][:, t, :],
-                    scalar1=state["d", g][:, t : t + 1],
-                    scalar2=0.0,
-                    op0=ALU.mult,
-                    op1=ALU.add,
-                )
-            state["half_a", g] = half_a
-
-        def scale_columns(g):
-            a_grouped = work.tile([P, NODES, PACK], BF16, name="a_grouped", align_bytes=64)
-            nc.vector.tensor_tensor(
-                out=a_grouped[:].rearrange("p (c i) t -> p c t i", i=4),
-                in0=state["half_a", g][:].rearrange("p t (c i) -> p c t i", i=4),
-                in1=state["d_all", g][:]
-                .rearrange("p (c i) -> p c i", i=4)
-                .unsqueeze(2)
-                .to_broadcast([P, NODES // 4, PACK, 4]),
-                op=ALU.mult,
-            )
-            state["a_grouped", g] = a_grouped
-
-        def regroup_msg(g):
-            msg_grouped = work.tile([P, HIDDEN, PACK], BF16, name="msg_grouped", align_bytes=64)
-            regroup(nc.scalar.copy, msg_grouped[:], msg_rows[g][:])
-            state["msg_grouped", g] = msg_grouped
-
-        def quantise_msg(g):
-            msg_codes = work.tile([P, HIDDEN], U32, name="msg_codes", align_bytes=64)
-            msg_scales = work.tile([P, HIDDEN], U8, name="msg_scales", align_bytes=64)
-            quantise(nc, msg_codes[:], msg_scales[:], state["msg_grouped", g][:])
-            state["msg_codes", g] = msg_codes
-            state["msg_scales", g] = msg_scales
-
-        def aggregate(g):
-            a_codes = work.tile([P, NODES], U32, name="a_codes", align_bytes=64)
-            a_scales = work.tile([P, NODES], U8, name="a_scales", align_bytes=64)
-            quantise(nc, a_codes[:], a_scales[:], state["a_grouped", g][:])
-            sums = []
-            for t in range(PACK):
-                f_cols = slice(t * P, (t + 1) * P)
-                sums_t = psum_h.tile([P, NODES], F32, name="sums", tag="sums")
-                nc.tensor.matmul_mx(
-                    out=sums_t[:],
-                    lhsT=state["msg_codes", g][:, f_cols].bitcast(FP8X4),
-                    lhsT_scale=state["msg_scales", g][:, f_cols],
-                    rhs=a_codes[:].bitcast(FP8X4),
-                    rhs_scale=a_scales[:],
-                    start=True,
-                    stop=True,
-                )
-                sums.append(sums_t)
-            state["sums", g] = sums
-
-        def bias_relu(g):
-            h_rows = work.tile([P, PACK, NODES], BF16, name="h_rows")
-            for t in range(PACK):
-                nc.scalar.activation(
-                    out=h_rows[:, t, :],
-                    in_=state["sums", g][t][:],
-                    func=ACT.Relu,
-                    bias=bias[:, t : t + 1],
-                    scale=1.0,
-                )
-            state["h_rows", g] = h_rows
-
-        def regroup_h(g):
-            h_grouped = work.tile([P, NODES, PACK], BF16, name="h_grouped", align_bytes=64)
-            regroup(nc.vector.tensor_copy, h_grouped[:], state["h_rows", g][:])
-            state["h_grouped", g] = h_grouped
-
-        def project(g):
-            h_codes = work.tile([P, NODES], U32, name="h_codes", align_bytes=64)
-            h_scales = work.tile([P, NODES], U8, name="h_scales", align_bytes=64)
-            quantise(nc, h_codes[:], h_scales[:], state["h_grouped", g][:])
-            proj = psum_out.tile([P, PACK, OUT], F32, name="proj", tag="proj")
-            for s in range(PACK):
-                i_cols = slice(s * P, (s + 1) * P)
-                nc.tensor.matmul_mx(
-                    out=proj[:, s, :],
-                    lhsT=h_codes[:, i_cols].bitcast(FP8X4),
-                    lhsT_scale=h_scales[:, i_cols],
-                    rhs=w3_codes[:].bitcast(FP8X4),
-                    rhs_scale=w3_scales[:],
-                    start=True,
-                    stop=True,
-                )
-            state["proj", g] = proj
-
-        def store(g):
-            result = work.tile([P, PACK, OUT], F32, name="result")
-            nc.scalar.copy(out=result[:], in_=state["proj", g][:])
-            nc.sync.dma_start(out=out[g].rearrange("(s p) o -> p s o", p=P), in_=result[:])
-
-        def live(g):
-            return 0 <= g < GRAPHS
-
-        def step(k):
-            if live(k):
-                scale_columns(k)
-            if live(k + 1):
-                scale_rows(k + 1)
-            if live(k + 2):
-                degrees(k + 2)
-            if live(k - 1):
-                bias_relu(k - 1)
-            if live(k + 2):
-                floor_degrees(k + 2)
-                inverse_root(k + 2)
-            if live(k - 2):
-                project(k - 2)
-            if live(k + 1):
-                quantise_msg(k + 1)
-            if live(k):
-                aggregate(k)
-            if live(k + 2):
-                regroup_msg(k + 2)
-            if live(k - 2):
-                store(k - 2)
-            if live(k - 1):
-                regroup_h(k - 1)
-            if live(k + 2):
-                spread_d(k + 2)
-
-        step(-2)
-        step(-1)
 
         b2_rows_f32 = const.tile([P, P], F32)
         nc.vector.tensor_copy(out=b2_rows_f32[:], in_=b2_rows[:])
@@ -261,5 +96,167 @@ def tile_perception_pb_t_kernel(tc, msg, adj, b2, W3, out):
         w3_scales = const.tile([P, OUT], U8, align_bytes=64)
         quantise(nc, w3_codes[:], w3_scales[:], w3_grouped[:])
 
-        for k in range(GRAPHS + 2):
-            step(k)
+        tiles = {}
+
+        def sum_degrees(g):
+            deg = psum_deg.tile([P, PACK, ONES_COLS], F32, name="deg")
+            for s in range(PACK):
+                for t in range(PACK):
+                    nc.tensor.matmul(
+                        out=deg[:, s, :],
+                        lhsT=adj_rows[g][:, t, s * P : (s + 1) * P],
+                        rhs=ones[:],
+                        start=(t == 0),
+                        stop=(t == PACK - 1),
+                    )
+            tiles["deg", g] = deg
+
+        def floor_degrees(g):
+            floored = work.tile([P, PACK], F32, name="floored")
+            nc.vector.tensor_scalar_max(out=floored[:], in0=tiles["deg", g][:, :, 0], scalar1=1e-30)
+            tiles["floored", g] = floored
+
+        def inverse_root(g):
+            root = work.tile([P, PACK], F32, name="root")
+            nc.scalar.activation(out=root[:], in_=tiles["floored", g][:], func=ACT.Abs_reciprocal_sqrt)
+            tiles["root", g] = root
+
+        def mask_d(g):
+            d = work.tile([P, PACK], F32, name="d")
+            nc.vector.scalar_tensor_tensor(
+                out=d[:],
+                in0=tiles["deg", g][:, :, 0],
+                scalar=0.0,
+                in1=tiles["root", g][:],
+                op0=ALU.is_gt,
+                op1=ALU.mult,
+            )
+            tiles["d", g] = d
+
+        def spread_d(g):
+            d_all = psum_bcast.tile([P, NODES], F32, name="d_all")
+            for t in range(PACK):
+                nc.tensor.transpose(
+                    d_all[:, t * P : (t + 1) * P],
+                    tiles["d", g][:, t : t + 1].to_broadcast([P, P]),
+                    ident[:],
+                )
+            tiles["d_all", g] = d_all
+
+        def scale_rows(g):
+            half_a = work.tile([P, PACK, NODES], F32, name="half_a")
+            for t in range(PACK):
+                nc.gpsimd.tensor_scalar(
+                    out=half_a[:, t, :],
+                    in0=adj_rows[g][:, t, :],
+                    scalar1=tiles["d", g][:, t : t + 1],
+                    scalar2=0.0,
+                    op0=ALU.mult,
+                    op1=ALU.add,
+                )
+            tiles["half_a", g] = half_a
+
+        def scale_columns(g):
+            a_grouped = work.tile([P, NODES, PACK], BF16, name="a_grouped", align_bytes=64)
+            nc.vector.tensor_tensor(
+                out=by_runs_grouped(a_grouped[:]),
+                in0=by_runs_rows(tiles["half_a", g][:]),
+                in1=tiles["d_all", g][:]
+                .rearrange("p (c i) -> p c i", i=RUN)
+                .unsqueeze(2)
+                .to_broadcast([P, NODES // RUN, PACK, RUN]),
+                op=ALU.mult,
+            )
+            tiles["a_grouped", g] = a_grouped
+
+        def regroup_msg(g):
+            msg_grouped = ahead.tile([P, HIDDEN, PACK], BF16, name="msg_grouped", align_bytes=64)
+            regroup(nc.scalar.copy, msg_grouped[:], msg_rows[g][:])
+            tiles["msg_grouped", g] = msg_grouped
+
+        def quantise_msg(g):
+            msg_codes = work.tile([P, HIDDEN], U32, name="msg_codes", align_bytes=64)
+            msg_scales = work.tile([P, HIDDEN], U8, name="msg_scales", align_bytes=64)
+            quantise(nc, msg_codes[:], msg_scales[:], tiles["msg_grouped", g][:])
+            tiles["msg_codes", g] = msg_codes
+            tiles["msg_scales", g] = msg_scales
+
+        def aggregate(g):
+            a_codes = work.tile([P, NODES], U32, name="a_codes", align_bytes=64)
+            a_scales = work.tile([P, NODES], U8, name="a_scales", align_bytes=64)
+            quantise(nc, a_codes[:], a_scales[:], tiles["a_grouped", g][:])
+            sums = []
+            for t in range(PACK):
+                f_cols = slice(t * P, (t + 1) * P)
+                sums_t = psum_h.tile([P, NODES], F32, name="sums", tag="sums")
+                nc.tensor.matmul_mx(
+                    out=sums_t[:],
+                    lhsT=tiles["msg_codes", g][:, f_cols].bitcast(FP8X4),
+                    lhsT_scale=tiles["msg_scales", g][:, f_cols],
+                    rhs=a_codes[:].bitcast(FP8X4),
+                    rhs_scale=a_scales[:],
+                    start=True,
+                    stop=True,
+                )
+                sums.append(sums_t)
+            tiles["sums", g] = sums
+
+        def bias_relu(g):
+            h_rows = work.tile([P, PACK, NODES], BF16, name="h_rows")
+            for t in range(PACK):
+                nc.scalar.activation(
+                    out=h_rows[:, t, :],
+                    in_=tiles["sums", g][t][:],
+                    func=ACT.Relu,
+                    bias=bias[:, t : t + 1],
+                    scale=1.0,
+                )
+            tiles["h_rows", g] = h_rows
+
+        def regroup_h(g):
+            h_grouped = work.tile([P, NODES, PACK], BF16, name="h_grouped", align_bytes=64)
+            regroup(nc.vector.tensor_copy, h_grouped[:], tiles["h_rows", g][:])
+            tiles["h_grouped", g] = h_grouped
+
+        def project(g):
+            h_codes = work.tile([P, NODES], U32, name="h_codes", align_bytes=64)
+            h_scales = work.tile([P, NODES], U8, name="h_scales", align_bytes=64)
+            quantise(nc, h_codes[:], h_scales[:], tiles["h_grouped", g][:])
+            proj = psum_out.tile([P, PACK, OUT], F32, name="proj", tag="proj")
+            for s in range(PACK):
+                i_cols = slice(s * P, (s + 1) * P)
+                nc.tensor.matmul_mx(
+                    out=proj[:, s, :],
+                    lhsT=h_codes[:, i_cols].bitcast(FP8X4),
+                    lhsT_scale=h_scales[:, i_cols],
+                    rhs=w3_codes[:].bitcast(FP8X4),
+                    rhs_scale=w3_scales[:],
+                    start=True,
+                    stop=True,
+                )
+            tiles["proj", g] = proj
+
+        def store(g):
+            result = work.tile([P, PACK, OUT], F32, name="result")
+            nc.scalar.copy(out=result[:], in_=tiles["proj", g][:])
+            nc.sync.dma_start(out=out[g].rearrange("(s p) o -> p s o", p=P), in_=result[:])
+
+        def run(stage, g):
+            if 0 <= g < GRAPHS:
+                stage(g)
+
+        for k in range(-3, GRAPHS + 3):
+            run(scale_columns, k)
+            run(scale_rows, k + 1)
+            run(sum_degrees, k + 3)
+            run(spread_d, k + 1)
+            run(bias_relu, k - 1)
+            run(floor_degrees, k + 3)
+            run(inverse_root, k + 3)
+            run(project, k - 3)
+            run(quantise_msg, k + 1)
+            run(aggregate, k)
+            run(regroup_msg, k + 3)
+            run(store, k - 3)
+            run(regroup_h, k - 2)
+            run(mask_d, k + 2)

@@ -83,19 +83,6 @@ def tile_perception_pb_t_kernel(tc, msg, adj, b2, W3, out):
         ones = const.tile([P, ONES_COLS], BF16)
         nc.vector.memset(ones[:], 1.0)
 
-        b2_rows_f32 = const.tile([P, P], F32)
-        nc.vector.tensor_copy(out=b2_rows_f32[:], in_=b2_rows[:])
-        b2_cols = psum_out.tile([P, PACK, OUT], F32, tag="proj")
-        nc.tensor.transpose(b2_cols[:, 0, :], b2_rows_f32[:], ident[:])
-        bias = const.tile([P, PACK], F32)
-        nc.vector.tensor_copy(out=bias[:], in_=b2_cols[:, 0, 0:PACK])
-
-        w3_grouped = const.tile([P, OUT, PACK], BF16, align_bytes=64)
-        regroup(nc.vector.tensor_copy, w3_grouped[:], w3_rows[:])
-        w3_codes = const.tile([P, OUT], U32, align_bytes=64)
-        w3_scales = const.tile([P, OUT], U8, align_bytes=64)
-        quantise(nc, w3_codes[:], w3_scales[:], w3_grouped[:])
-
         tiles = {}
 
         def sum_degrees(g):
@@ -245,7 +232,7 @@ def tile_perception_pb_t_kernel(tc, msg, adj, b2, W3, out):
             if 0 <= g < GRAPHS:
                 stage(g)
 
-        for k in range(-3, GRAPHS + 3):
+        def step(k):
             run(scale_columns, k)
             run(scale_rows, k + 1)
             run(sum_degrees, k + 3)
@@ -260,3 +247,22 @@ def tile_perception_pb_t_kernel(tc, msg, adj, b2, W3, out):
             run(store, k - 3)
             run(regroup_h, k - 2)
             run(mask_d, k + 2)
+
+        for k in range(-3, -1):
+            step(k)
+
+        b2_rows_f32 = const.tile([P, P], F32)
+        nc.vector.tensor_copy(out=b2_rows_f32[:], in_=b2_rows[:])
+        b2_cols = psum_out.tile([P, PACK, OUT], F32, tag="proj")
+        nc.tensor.transpose(b2_cols[:, 0, :], b2_rows_f32[:], ident[:])
+        bias = const.tile([P, PACK], F32)
+        nc.vector.tensor_copy(out=bias[:], in_=b2_cols[:, 0, 0:PACK])
+
+        w3_grouped = const.tile([P, OUT, PACK], BF16, align_bytes=64)
+        regroup(nc.vector.tensor_copy, w3_grouped[:], w3_rows[:])
+        w3_codes = const.tile([P, OUT], U32, align_bytes=64)
+        w3_scales = const.tile([P, OUT], U8, align_bytes=64)
+        quantise(nc, w3_codes[:], w3_scales[:], w3_grouped[:])
+
+        for k in range(-1, GRAPHS + 3):
+            step(k)

@@ -17,16 +17,22 @@ NODES = 512
 HIDDEN = 512
 OUT = 128
 ONES_COLS = 32
+DEG_GROUPS = ((0,), (1,), (2, 3), (4, 5, 6, 7), (8, 9, 10, 11), (12, 13, 14, 15))
+DEG_MAX = 4
 
 FLOPS = 2 * GRAPHS * (NODES * NODES * HIDDEN + NODES * HIDDEN * OUT)
+
+
+def degree_step(g):
+    return max(g // 2 - 1, g - 5)
 
 
 def by_runs_grouped(grouped):
     return grouped.rearrange("p (c i) t -> p c t i", i=RUN)
 
 
-def by_runs_rows(rows):
-    return rows.rearrange("p t (c i) -> p c t i", i=RUN)
+def by_runs_rows(planes):
+    return planes.rearrange("p t (c i) -> p c t i", i=RUN)
 
 
 def regroup(copy, grouped, rows):
@@ -48,6 +54,7 @@ def tile_perception_pb_t_kernel(tc, msg, adj, b2, W3, out):
         tc.tile_pool(name="inputs", bufs=1) as inputs,
         tc.tile_pool(name="work", bufs=2) as work,
         tc.tile_pool(name="ahead", bufs=3) as ahead,
+        tc.tile_pool(name="rows", bufs=5) as rows,
         tc.psum_pool(name="psum_deg", bufs=2) as psum_deg,
         tc.psum_pool(name="psum_bcast", bufs=1) as psum_bcast,
         tc.psum_pool(name="psum_h", bufs=PACK) as psum_h,
@@ -73,52 +80,63 @@ def tile_perception_pb_t_kernel(tc, msg, adj, b2, W3, out):
             msg_rows.append(msg_g)
 
         load_adj(0)
-        for g in range(GRAPHS):
-            if g + 1 < GRAPHS:
-                load_adj(g + 1)
-            load_msg(g)
+        load_msg(0)
+        for k in range(-1, GRAPHS):
+            for g in range(1, GRAPHS):
+                if degree_step(g) == k:
+                    load_adj(g)
+            if k + 2 < GRAPHS:
+                load_msg(k + 2)
 
         ident = const.tile([P, P], F32)
         make_identity(nc, ident[:])
         ones = const.tile([P, ONES_COLS], BF16)
         nc.vector.memset(ones[:], 1.0)
+        floor = const.tile([P, 1], F32)
+        nc.vector.memset(floor[:], 1e-30)
 
         tiles = {}
 
         def sum_degrees(g):
-            deg = psum_deg.tile([P, PACK, ONES_COLS], F32, name="deg")
+            for group in DEG_GROUPS:
+                if g == group[0]:
+                    tiles["deg", group] = psum_deg.tile([P, DEG_MAX, PACK, ONES_COLS], F32, name="deg")
+                if g in group:
+                    deg = tiles["deg", group]
+                    n = group.index(g)
             for s in range(PACK):
                 for t in range(PACK):
                     nc.tensor.matmul(
-                        out=deg[:, s, :],
+                        out=deg[:, n, s, :],
                         lhsT=adj_rows[g][:, t, s * P : (s + 1) * P],
                         rhs=ones[:],
                         start=(t == 0),
                         stop=(t == PACK - 1),
                     )
-            tiles["deg", g] = deg
 
-        def floor_degrees(g):
-            floored = work.tile([P, PACK], F32, name="floored")
-            nc.vector.tensor_scalar_max(out=floored[:], in0=tiles["deg", g][:, :, 0], scalar1=1e-30)
-            tiles["floored", g] = floored
+        def inverse_root(group):
+            root = work.tile([P, DEG_MAX, PACK], F32, name="root")
+            nc.scalar.activation(
+                out=root[:, 0 : len(group), :],
+                in_=tiles["deg", group][:, 0 : len(group), :, 0],
+                func=ACT.Abs_reciprocal_sqrt,
+                bias=floor[:],
+                scale=1.0,
+            )
+            tiles["root", group] = root
 
-        def inverse_root(g):
-            root = work.tile([P, PACK], F32, name="root")
-            nc.scalar.activation(out=root[:], in_=tiles["floored", g][:], func=ACT.Abs_reciprocal_sqrt)
-            tiles["root", g] = root
-
-        def mask_d(g):
-            d = work.tile([P, PACK], F32, name="d")
+        def mask_d(group):
+            d = work.tile([P, DEG_MAX, PACK], F32, name="d")
             nc.vector.scalar_tensor_tensor(
-                out=d[:],
-                in0=tiles["deg", g][:, :, 0],
+                out=d[:, 0 : len(group), :],
+                in0=tiles["deg", group][:, 0 : len(group), :, 0],
                 scalar=0.0,
-                in1=tiles["root", g][:],
+                in1=tiles["root", group][:, 0 : len(group), :],
                 op0=ALU.is_gt,
                 op1=ALU.mult,
             )
-            tiles["d", g] = d
+            for n, g in enumerate(group):
+                tiles["d", g] = d[:, n, :]
 
         def spread_d(g):
             d_all = psum_bcast.tile([P, NODES], F32, name="d_all")
@@ -131,7 +149,7 @@ def tile_perception_pb_t_kernel(tc, msg, adj, b2, W3, out):
             tiles["d_all", g] = d_all
 
         def scale_rows(g):
-            half_a = work.tile([P, PACK, NODES], F32, name="half_a")
+            half_a = rows.tile([P, PACK, NODES], F32, name="half_a", tag="rows")
             for t in range(PACK):
                 nc.gpsimd.tensor_scalar(
                     out=half_a[:, t, :],
@@ -189,7 +207,7 @@ def tile_perception_pb_t_kernel(tc, msg, adj, b2, W3, out):
             tiles["sums", g] = sums
 
         def bias_relu(g):
-            h_rows = work.tile([P, PACK, NODES], BF16, name="h_rows")
+            h_rows = rows.tile([P, PACK, NODES], BF16, name="h_rows", tag="rows")
             for t in range(PACK):
                 nc.scalar.activation(
                     out=h_rows[:, t, :],
@@ -232,24 +250,39 @@ def tile_perception_pb_t_kernel(tc, msg, adj, b2, W3, out):
             if 0 <= g < GRAPHS:
                 stage(g)
 
+        def run_groups(stage, k):
+            for group in DEG_GROUPS:
+                if degree_step(group[-1]) == k:
+                    stage(group)
+
         def step(k):
             run(scale_columns, k)
-            run(scale_rows, k + 1)
-            run(sum_degrees, k + 3)
+            for g in range(GRAPHS):
+                if degree_step(g) == k and k >= 0:
+                    sum_degrees(g)
             run(spread_d, k + 1)
             run(bias_relu, k - 1)
-            run(floor_degrees, k + 3)
-            run(inverse_root, k + 3)
+            run(scale_rows, k + 1)
+            run_groups(inverse_root, k)
             run(project, k - 3)
             run(quantise_msg, k + 1)
             run(aggregate, k)
-            run(regroup_msg, k + 3)
+            run(regroup_msg, k + 2)
             run(store, k - 3)
             run(regroup_h, k - 2)
-            run(mask_d, k + 2)
+            run_groups(mask_d, k)
 
-        for k in range(-3, -1):
-            step(k)
+        sum_degrees(0)
+        inverse_root((0,))
+        mask_d((0,))
+        spread_d(0)
+        scale_rows(0)
+        regroup_msg(0)
+        sum_degrees(1)
+        inverse_root((1,))
+        mask_d((1,))
+        quantise_msg(0)
+        regroup_msg(1)
 
         b2_rows_f32 = const.tile([P, P], F32)
         nc.vector.tensor_copy(out=b2_rows_f32[:], in_=b2_rows[:])
@@ -264,5 +297,5 @@ def tile_perception_pb_t_kernel(tc, msg, adj, b2, W3, out):
         w3_scales = const.tile([P, OUT], U8, align_bytes=64)
         quantise(nc, w3_codes[:], w3_scales[:], w3_grouped[:])
 
-        for k in range(-1, GRAPHS + 3):
+        for k in range(GRAPHS + 3):
             step(k)

@@ -16,6 +16,7 @@ GRAPHS = 16
 NODES = 512
 HIDDEN = 512
 OUT = 128
+GPSIMD_ROWS = 3
 ONES_COLS = 32
 DEG_GROUPS = ((0,), (1,), (2, 3), (4, 5, 6, 7), (8, 9, 10, 11), (12, 13, 14, 15))
 DEG_MAX = 4
@@ -150,7 +151,7 @@ def tile_perception_pb_t_kernel(tc, msg, adj, b2, W3, out):
 
         def scale_rows(g):
             half_a = rows.tile([P, PACK, NODES], F32, name="half_a", tag="rows")
-            for t in range(PACK):
+            for t in range(GPSIMD_ROWS):
                 nc.gpsimd.tensor_scalar(
                     out=half_a[:, t, :],
                     in0=adj_rows[g][:, t, :],
@@ -160,6 +161,14 @@ def tile_perception_pb_t_kernel(tc, msg, adj, b2, W3, out):
                     op1=ALU.add,
                 )
             tiles["half_a", g] = half_a
+
+        def scale_last_rows(g):
+            for t in range(GPSIMD_ROWS, PACK):
+                nc.vector.tensor_scalar_mul(
+                    out=tiles["half_a", g][:, t, :],
+                    in0=adj_rows[g][:, t, :],
+                    scalar1=tiles["d", g][:, t : t + 1],
+                )
 
         def scale_columns(g):
             a_grouped = work.tile([P, NODES, PACK], BF16, name="a_grouped", align_bytes=64)
@@ -265,6 +274,7 @@ def tile_perception_pb_t_kernel(tc, msg, adj, b2, W3, out):
             run(scale_rows, k + 1)
             run_groups(inverse_root, k)
             run(project, k - 3)
+            run(scale_last_rows, k + 1)
             run(quantise_msg, k + 1)
             run(aggregate, k)
             run(regroup_msg, k + 2)
@@ -281,6 +291,7 @@ def tile_perception_pb_t_kernel(tc, msg, adj, b2, W3, out):
         sum_degrees(1)
         inverse_root((1,))
         mask_d((1,))
+        scale_last_rows(0)
         quantise_msg(0)
         regroup_msg(1)
 

@@ -16,16 +16,19 @@ GRAPHS = 16
 NODES = 512
 HIDDEN = 512
 OUT = 128
-GPSIMD_ROWS = 3
-ONES_COLS = 32
-DEG_GROUPS = ((0,), (1,), (2, 3), (4, 5, 6, 7), (8, 9, 10, 11), (12, 13, 14, 15))
-DEG_MAX = 4
+ROW_ENGINES = "GGGM"
+VECTOR_COLS = 256
+ONES_COLS = 48
+DEG_GROUPS = ((0,), (1,), (2,), (3,), (4, 5), (6, 7), (8, 9), (10, 11), (12, 13), (14, 15))
+WARM_COLS = 512
+WARM = 7
+DEG_MAX = 2
 
 FLOPS = 2 * GRAPHS * (NODES * NODES * HIDDEN + NODES * HIDDEN * OUT)
 
 
-def degree_step(g):
-    return max(g // 2 - 1, g - 5)
+def mask_step(group):
+    return max(group[-1] - 3, 1)
 
 
 def by_runs_grouped(grouped):
@@ -62,11 +65,6 @@ def tile_perception_pb_t_kernel(tc, msg, adj, b2, W3, out):
         tc.psum_pool(name="psum_out", bufs=1) as psum_out,
         tc.manual_schedule(),
     ):
-        b2_rows = const.tile([P, P], BF16)
-        nc.vector.memset(b2_rows[:], 0.0)
-        nc.scalar.dma_start(out=b2_rows[0:PACK, :], in_=b2.rearrange("(t p) -> t p", p=P))
-        w3_rows = const.tile([P, PACK, OUT], BF16)
-        nc.scalar.dma_start(out=w3_rows[:], in_=W3.rearrange("(t p) o -> p t o", p=P))
         adj_rows = []
         msg_rows = []
 
@@ -81,20 +79,28 @@ def tile_perception_pb_t_kernel(tc, msg, adj, b2, W3, out):
             msg_rows.append(msg_g)
 
         load_adj(0)
-        load_msg(0)
-        for k in range(-1, GRAPHS):
-            for g in range(1, GRAPHS):
-                if degree_step(g) == k:
-                    load_adj(g)
-            if k + 2 < GRAPHS:
-                load_msg(k + 2)
+        w3_rows = const.tile([P, PACK, OUT], BF16)
+        nc.sync.dma_start(out=w3_rows[:], in_=W3.rearrange("(t p) o -> p t o", p=P))
+        b2_rows = const.tile([P, P], BF16)
+        nc.vector.memset(b2_rows[:], 0.0)
+        nc.sync.dma_start(out=b2_rows[0:PACK, :], in_=b2.rearrange("(t p) -> t p", p=P))
+        load_adj(1)
+        for g in range(GRAPHS):
+            load_msg(g)
+            if g + 2 < GRAPHS:
+                load_adj(g + 2)
 
-        ident = const.tile([P, P], F32)
-        make_identity(nc, ident[:])
         ones = const.tile([P, ONES_COLS], BF16)
         nc.vector.memset(ones[:], 1.0)
+        blank = const.tile([P, WARM_COLS], BF16)
+        nc.gpsimd.memset(blank[:], 0.0)
         floor = const.tile([P, 1], F32)
         nc.vector.memset(floor[:], 1e-30)
+        ident = const.tile([P, P], F32)
+        make_identity(nc, ident[:])
+        for n in range(WARM):
+            idle = psum_h.tile([P, WARM_COLS], F32, name="idle", tag="sums")
+            nc.tensor.matmul(out=idle[:], lhsT=blank[:, 0:P], rhs=blank[:], start=True, stop=True)
 
         tiles = {}
 
@@ -149,26 +155,27 @@ def tile_perception_pb_t_kernel(tc, msg, adj, b2, W3, out):
                 )
             tiles["d_all", g] = d_all
 
-        def scale_rows(g):
-            half_a = rows.tile([P, PACK, NODES], F32, name="half_a", tag="rows")
-            for t in range(GPSIMD_ROWS):
-                nc.gpsimd.tensor_scalar(
-                    out=half_a[:, t, :],
-                    in0=adj_rows[g][:, t, :],
-                    scalar1=tiles["d", g][:, t : t + 1],
-                    scalar2=0.0,
-                    op0=ALU.mult,
-                    op1=ALU.add,
-                )
-            tiles["half_a", g] = half_a
+        def new_half_a(g):
+            tiles["half_a", g] = rows.tile([P, PACK, NODES], F32, name="half_a", tag="rows")
 
-        def scale_last_rows(g):
-            for t in range(GPSIMD_ROWS, PACK):
-                nc.vector.tensor_scalar_mul(
-                    out=tiles["half_a", g][:, t, :],
-                    in0=adj_rows[g][:, t, :],
-                    scalar1=tiles["d", g][:, t : t + 1],
-                )
+        def scale_rows(g, engine, engines=ROW_ENGINES):
+            for t in range(PACK):
+                cols = slice(0, NODES)
+                if engines[t] == "M" and engine != "G":
+                    cols = slice(0, VECTOR_COLS) if engine == "V" else slice(VECTOR_COLS, NODES)
+                elif engines[t] != engine:
+                    continue
+                out = tiles["half_a", g][:, t, cols]
+                in0 = adj_rows[g][:, t, cols]
+                d_t = tiles["d", g][:, t : t + 1]
+                if engine == "G":
+                    nc.gpsimd.tensor_scalar(
+                        out=out, in0=in0, scalar1=d_t, scalar2=0.0, op0=ALU.mult, op1=ALU.add
+                    )
+                elif engine == "V":
+                    nc.vector.tensor_scalar_mul(out=out, in0=in0, scalar1=d_t)
+                else:
+                    nc.scalar.activation(out=out, in_=in0, func=ACT.Copy, scale=d_t)
 
         def scale_columns(g):
             a_grouped = work.tile([P, NODES, PACK], BF16, name="a_grouped", align_bytes=64)
@@ -183,9 +190,9 @@ def tile_perception_pb_t_kernel(tc, msg, adj, b2, W3, out):
             )
             tiles["a_grouped", g] = a_grouped
 
-        def regroup_msg(g):
+        def regroup_msg(g, copy=nc.scalar.copy):
             msg_grouped = ahead.tile([P, HIDDEN, PACK], BF16, name="msg_grouped", align_bytes=64)
-            regroup(nc.scalar.copy, msg_grouped[:], msg_rows[g][:])
+            regroup(copy, msg_grouped[:], msg_rows[g][:])
             tiles["msg_grouped", g] = msg_grouped
 
         def quantise_msg(g):
@@ -195,10 +202,14 @@ def tile_perception_pb_t_kernel(tc, msg, adj, b2, W3, out):
             tiles["msg_codes", g] = msg_codes
             tiles["msg_scales", g] = msg_scales
 
-        def aggregate(g):
+        def quantise_a(g):
             a_codes = work.tile([P, NODES], U32, name="a_codes", align_bytes=64)
             a_scales = work.tile([P, NODES], U8, name="a_scales", align_bytes=64)
             quantise(nc, a_codes[:], a_scales[:], tiles["a_grouped", g][:])
+            tiles["a_codes", g] = a_codes
+            tiles["a_scales", g] = a_scales
+
+        def aggregate(g):
             sums = []
             for t in range(PACK):
                 f_cols = slice(t * P, (t + 1) * P)
@@ -207,8 +218,8 @@ def tile_perception_pb_t_kernel(tc, msg, adj, b2, W3, out):
                     out=sums_t[:],
                     lhsT=tiles["msg_codes", g][:, f_cols].bitcast(FP8X4),
                     lhsT_scale=tiles["msg_scales", g][:, f_cols],
-                    rhs=a_codes[:].bitcast(FP8X4),
-                    rhs_scale=a_scales[:],
+                    rhs=tiles["a_codes", g][:].bitcast(FP8X4),
+                    rhs_scale=tiles["a_scales", g][:],
                     start=True,
                     stop=True,
                 )
@@ -218,6 +229,16 @@ def tile_perception_pb_t_kernel(tc, msg, adj, b2, W3, out):
         def bias_relu(g):
             h_rows = rows.tile([P, PACK, NODES], BF16, name="h_rows", tag="rows")
             for t in range(PACK):
+                if g == GRAPHS - 1 and t >= 2:
+                    nc.vector.tensor_scalar(
+                        out=h_rows[:, t, :],
+                        in0=tiles["sums", g][t][:],
+                        scalar1=bias[:, t : t + 1],
+                        scalar2=0.0,
+                        op0=ALU.add,
+                        op1=ALU.max,
+                    )
+                    continue
                 nc.scalar.activation(
                     out=h_rows[:, t, :],
                     in_=tiles["sums", g][t][:],
@@ -229,7 +250,10 @@ def tile_perception_pb_t_kernel(tc, msg, adj, b2, W3, out):
 
         def regroup_h(g):
             h_grouped = work.tile([P, NODES, PACK], BF16, name="h_grouped", align_bytes=64)
-            regroup(nc.vector.tensor_copy, h_grouped[:], tiles["h_rows", g][:])
+            split = NODES if g < GRAPHS - 2 else 320
+            regroup(nc.vector.tensor_copy, h_grouped[:, 0:split, :], tiles["h_rows", g][:, :, 0:split])
+            if split < NODES:
+                regroup(nc.scalar.copy, h_grouped[:, split:, :], tiles["h_rows", g][:, :, split:])
             tiles["h_grouped", g] = h_grouped
 
         def project(g):
@@ -261,52 +285,74 @@ def tile_perception_pb_t_kernel(tc, msg, adj, b2, W3, out):
 
         def run_groups(stage, k):
             for group in DEG_GROUPS:
-                if degree_step(group[-1]) == k:
-                    stage(group)
+                if len(group) > 1 or group == (3,):
+                    if mask_step(group) == k:
+                        stage(group)
 
         def step(k):
             run(scale_columns, k)
-            for g in range(GRAPHS):
-                if degree_step(g) == k and k >= 0:
-                    sum_degrees(g)
             run(spread_d, k + 1)
+            if k == 1:
+                sum_degrees(4)
+            run(sum_degrees, k + 4)
+            if k > 1:
+                run_groups(inverse_root, k)
             run(bias_relu, k - 1)
-            run(scale_rows, k + 1)
-            run_groups(inverse_root, k)
+            if k == 1:
+                run_groups(inverse_root, k)
+            run(new_half_a, k + 1)
+            engines = ROW_ENGINES if k > 1 else "GGGV"
+            if k + 1 < GRAPHS:
+                scale_rows(k + 1, "G", engines)
+                scale_rows(k + 1, "S", engines)
             run(project, k - 3)
-            run(scale_last_rows, k + 1)
-            run(quantise_msg, k + 1)
+            if k + 1 < GRAPHS:
+                scale_rows(k + 1, "V", engines)
+            run(quantise_msg, k)
+            run(quantise_a, k)
             run(aggregate, k)
-            run(regroup_msg, k + 2)
-            run(store, k - 3)
+            run(regroup_msg, k + 1)
+            if k < GRAPHS:
+                run(store, k - 3)
             run(regroup_h, k - 2)
+            if k >= GRAPHS:
+                run(store, k - 3)
             run_groups(mask_d, k)
 
         sum_degrees(0)
         inverse_root((0,))
-        mask_d((0,))
-        spread_d(0)
-        scale_rows(0)
-        regroup_msg(0)
-        sum_degrees(1)
-        inverse_root((1,))
-        mask_d((1,))
-        scale_last_rows(0)
-        quantise_msg(0)
-        regroup_msg(1)
-
-        b2_rows_f32 = const.tile([P, P], F32)
-        nc.vector.tensor_copy(out=b2_rows_f32[:], in_=b2_rows[:])
-        b2_cols = psum_out.tile([P, PACK, OUT], F32, tag="proj")
-        nc.tensor.transpose(b2_cols[:, 0, :], b2_rows_f32[:], ident[:])
-        bias = const.tile([P, PACK], F32)
-        nc.vector.tensor_copy(out=bias[:], in_=b2_cols[:, 0, 0:PACK])
-
         w3_grouped = const.tile([P, OUT, PACK], BF16, align_bytes=64)
         regroup(nc.vector.tensor_copy, w3_grouped[:], w3_rows[:])
+        b2_rows_f32 = const.tile([P, P], F32)
+        nc.vector.tensor_copy(out=b2_rows_f32[:], in_=b2_rows[:])
         w3_codes = const.tile([P, OUT], U32, align_bytes=64)
         w3_scales = const.tile([P, OUT], U8, align_bytes=64)
         quantise(nc, w3_codes[:], w3_scales[:], w3_grouped[:])
+        mask_d((0,))
+        sum_degrees(1)
+        new_half_a(0)
+        for engine in "GVS":
+            scale_rows(0, engine, "VVVS")
+        spread_d(0)
+        b2_cols = psum_out.tile([P, PACK, OUT], F32, tag="proj", name="b2_cols")
+        nc.tensor.transpose(b2_cols[:, 0, :], b2_rows_f32[:], ident[:])
+        inverse_root((1,))
+        mask_d((1,))
+        scale_columns(0)
+        new_half_a(1)
+        scale_rows(1, "G", "GGGG")
+        regroup_msg(0)
+        sum_degrees(2)
+        bias = const.tile([P, PACK], F32)
+        nc.vector.tensor_copy(out=bias[:], in_=b2_cols[:, 0, 0:PACK])
+        quantise_msg(0)
+        quantise_a(0)
+        spread_d(1)
+        aggregate(0)
+        inverse_root((2,))
+        mask_d((2,))
+        regroup_msg(1)
+        sum_degrees(3)
 
-        for k in range(GRAPHS + 3):
+        for k in range(1, GRAPHS + 3):
             step(k)

@@ -59,6 +59,7 @@ def tile_perception_pb_t_kernel(tc, msg, adj, b2, W3, out):
         tc.tile_pool(name="work", bufs=2) as work,
         tc.tile_pool(name="ahead", bufs=3) as ahead,
         tc.tile_pool(name="rows", bufs=5) as rows,
+        tc.tile_pool(name="results", bufs=5) as results,
         tc.psum_pool(name="psum_deg", bufs=2) as psum_deg,
         tc.psum_pool(name="psum_bcast", bufs=1) as psum_bcast,
         tc.psum_pool(name="psum_h", bufs=PACK) as psum_h,
@@ -229,16 +230,6 @@ def tile_perception_pb_t_kernel(tc, msg, adj, b2, W3, out):
         def bias_relu(g):
             h_rows = rows.tile([P, PACK, NODES], BF16, name="h_rows", tag="rows")
             for t in range(PACK):
-                if g == GRAPHS - 1 and t >= 2:
-                    nc.vector.tensor_scalar(
-                        out=h_rows[:, t, :],
-                        in0=tiles["sums", g][t][:],
-                        scalar1=bias[:, t : t + 1],
-                        scalar2=0.0,
-                        op0=ALU.add,
-                        op1=ALU.max,
-                    )
-                    continue
                 nc.scalar.activation(
                     out=h_rows[:, t, :],
                     in_=tiles["sums", g][t][:],
@@ -248,20 +239,22 @@ def tile_perception_pb_t_kernel(tc, msg, adj, b2, W3, out):
                 )
             tiles["h_rows", g] = h_rows
 
-        def regroup_h(g):
-            h_grouped = work.tile([P, NODES, PACK], BF16, name="h_grouped", align_bytes=64)
-            split = NODES if g < GRAPHS - 2 else 320
-            regroup(nc.vector.tensor_copy, h_grouped[:, 0:split, :], tiles["h_rows", g][:, :, 0:split])
-            if split < NODES:
-                regroup(nc.scalar.copy, h_grouped[:, split:, :], tiles["h_rows", g][:, :, split:])
-            tiles["h_grouped", g] = h_grouped
+        def regroup_h(g, copy=nc.vector.tensor_copy, cols=slice(0, NODES)):
+            if ("h_grouped", g) not in tiles:
+                tiles["h_grouped", g] = work.tile(
+                    [P, NODES, PACK], BF16, name="h_grouped", align_bytes=64
+                )
+            regroup(copy, tiles["h_grouped", g][:, cols, :], tiles["h_rows", g][:, :, cols])
 
-        def project(g):
-            h_codes = work.tile([P, NODES], U32, name="h_codes", align_bytes=64)
-            h_scales = work.tile([P, NODES], U8, name="h_scales", align_bytes=64)
-            quantise(nc, h_codes[:], h_scales[:], tiles["h_grouped", g][:])
-            proj = psum_out.tile([P, PACK, OUT], F32, name="proj", tag="proj")
-            for s in range(PACK):
+        def project(g, part=0, parts=1, pool=psum_out, tag="proj"):
+            blocks = PACK // parts
+            first = part * blocks
+            cols = slice(first * P, (first + blocks) * P)
+            h_codes = work.tile([P, blocks * P], U32, name="h_codes", align_bytes=64)
+            h_scales = work.tile([P, blocks * P], U8, name="h_scales", align_bytes=64)
+            quantise(nc, h_codes[:], h_scales[:], tiles["h_grouped", g][:, cols, :])
+            proj = pool.tile([P, blocks, OUT], F32, name="proj", tag=tag)
+            for s in range(blocks):
                 i_cols = slice(s * P, (s + 1) * P)
                 nc.tensor.matmul_mx(
                     out=proj[:, s, :],
@@ -272,12 +265,14 @@ def tile_perception_pb_t_kernel(tc, msg, adj, b2, W3, out):
                     start=True,
                     stop=True,
                 )
-            tiles["proj", g] = proj
+            tiles["proj", g, part] = proj
 
-        def store(g):
-            result = work.tile([P, PACK, OUT], F32, name="result")
-            nc.scalar.copy(out=result[:], in_=tiles["proj", g][:])
-            nc.sync.dma_start(out=out[g].rearrange("(s p) o -> p s o", p=P), in_=result[:])
+        def store(g, part=0, parts=1, copy=nc.scalar.copy):
+            blocks = PACK // parts
+            nodes = slice(part * blocks * P, (part + 1) * blocks * P)
+            result = results.tile([P, blocks, OUT], F32, name="result")
+            copy(out=result[:], in_=tiles["proj", g, part][:])
+            nc.sync.dma_start(out=out[g, nodes].rearrange("(s p) o -> p s o", p=P), in_=result[:])
 
         def run(stage, g):
             if 0 <= g < GRAPHS:
@@ -292,16 +287,11 @@ def tile_perception_pb_t_kernel(tc, msg, adj, b2, W3, out):
         def step(k):
             run(scale_columns, k)
             run(spread_d, k + 1)
-            if k == 1:
-                sum_degrees(4)
-            run(sum_degrees, k + 4)
-            if k > 1:
-                run_groups(inverse_root, k)
+            run(sum_degrees, k + 4 if k > 1 else k + 3)
             run(bias_relu, k - 1)
-            if k == 1:
-                run_groups(inverse_root, k)
+            run_groups(inverse_root, k)
             run(new_half_a, k + 1)
-            engines = ROW_ENGINES if k > 1 else "GGGV"
+            engines = ROW_ENGINES if k > 2 else "GGGV"
             if k + 1 < GRAPHS:
                 scale_rows(k + 1, "G", engines)
                 scale_rows(k + 1, "S", engines)
@@ -311,12 +301,11 @@ def tile_perception_pb_t_kernel(tc, msg, adj, b2, W3, out):
             run(quantise_msg, k)
             run(quantise_a, k)
             run(aggregate, k)
+            if k == 1:
+                sum_degrees(k + 4)
             run(regroup_msg, k + 1)
-            if k < GRAPHS:
-                run(store, k - 3)
+            run(store, k - 3)
             run(regroup_h, k - 2)
-            if k >= GRAPHS:
-                run(store, k - 3)
             run_groups(mask_d, k)
 
         sum_degrees(0)
@@ -354,5 +343,30 @@ def tile_perception_pb_t_kernel(tc, msg, adj, b2, W3, out):
         regroup_msg(1)
         sum_degrees(3)
 
-        for k in range(1, GRAPHS + 3):
+        for k in range(1, GRAPHS - 1):
             step(k)
+
+        last = GRAPHS - 1
+        vector_cols = slice(0, 320)
+        scalar_cols = slice(320, NODES)
+        scale_columns(last)
+        bias_relu(last - 1)
+        quantise_msg(last)
+        quantise_a(last)
+        aggregate(last)
+        project(last - 3)
+        regroup_h(last - 1, nc.scalar.copy, scalar_cols)
+        regroup_h(last - 2)
+        regroup_h(last - 1, nc.vector.tensor_copy, vector_cols)
+        bias_relu(last)
+        project(last - 2, pool=psum_deg, tag="deg")
+        regroup_h(last, nc.vector.tensor_copy, vector_cols)
+        regroup_h(last, nc.scalar.copy, scalar_cols)
+        project(last - 1, pool=psum_deg, tag="deg")
+        project(last, 0, 2, psum_h, "sums")
+        project(last, 1, 2, psum_h, "sums")
+        store(last - 3)
+        store(last - 2)
+        store(last - 1)
+        store(last, 0, 2)
+        store(last, 1, 2, nc.vector.tensor_copy)

@@ -16,8 +16,10 @@ GRAPHS = 16
 NODES = 512
 HIDDEN = 512
 OUT = 128
-ROW_ENGINES = "GGGM"
-VECTOR_COLS = 256
+EARLY_SHARES = (("V", 0, 0, 512), ("V", 1, 0, 512), ("V", 2, 0, 512), ("S", 3, 0, 512))
+SECOND_SHARES = (("G", 0, 0, 512), ("G", 1, 0, 512), ("G", 2, 0, 512), ("S", 3, 0, 512))
+HEAD_SHARES = (("G", 0, 0, 512), ("G", 1, 0, 512), ("G", 2, 0, 512), ("V", 3, 0, 512))
+SHARES = (("G", 0, 0, 512), ("G", 1, 0, 512), ("G", 2, 0, 384), ("S", 2, 384, 512), ("V", 3, 0, 512))
 ONES_COLS = 48
 DEG_GROUPS = ((0,), (1,), (2,), (3,), (4, 5), (6, 7), (8, 9), (10, 11), (12, 13), (14, 15))
 WARM_COLS = 512
@@ -60,6 +62,7 @@ def tile_perception_pb_t_kernel(tc, msg, adj, b2, W3, out):
         tc.tile_pool(name="ahead", bufs=3) as ahead,
         tc.tile_pool(name="rows", bufs=5) as rows,
         tc.tile_pool(name="results", bufs=5) as results,
+        tc.tile_pool(name="h_mx", bufs=4) as h_mx,
         tc.psum_pool(name="psum_deg", bufs=2) as psum_deg,
         tc.psum_pool(name="psum_bcast", bufs=1) as psum_bcast,
         tc.psum_pool(name="psum_h", bufs=PACK) as psum_h,
@@ -159,15 +162,12 @@ def tile_perception_pb_t_kernel(tc, msg, adj, b2, W3, out):
         def new_half_a(g):
             tiles["half_a", g] = rows.tile([P, PACK, NODES], F32, name="half_a", tag="rows")
 
-        def scale_rows(g, engine, engines=ROW_ENGINES):
-            for t in range(PACK):
-                cols = slice(0, NODES)
-                if engines[t] == "M" and engine != "G":
-                    cols = slice(0, VECTOR_COLS) if engine == "V" else slice(VECTOR_COLS, NODES)
-                elif engines[t] != engine:
+        def scale_rows(g, engine, shares):
+            for name, t, first, end in shares:
+                if name != engine:
                     continue
-                out = tiles["half_a", g][:, t, cols]
-                in0 = adj_rows[g][:, t, cols]
+                out = tiles["half_a", g][:, t, first:end]
+                in0 = adj_rows[g][:, t, first:end]
                 d_t = tiles["d", g][:, t : t + 1]
                 if engine == "G":
                     nc.gpsimd.tensor_scalar(
@@ -250,8 +250,8 @@ def tile_perception_pb_t_kernel(tc, msg, adj, b2, W3, out):
             blocks = PACK // parts
             first = part * blocks
             cols = slice(first * P, (first + blocks) * P)
-            h_codes = work.tile([P, blocks * P], U32, name="h_codes", align_bytes=64)
-            h_scales = work.tile([P, blocks * P], U8, name="h_scales", align_bytes=64)
+            h_codes = h_mx.tile([P, blocks * P], U32, name="h_codes", align_bytes=64)
+            h_scales = h_mx.tile([P, blocks * P], U8, name="h_scales", align_bytes=64)
             quantise(nc, h_codes[:], h_scales[:], tiles["h_grouped", g][:, cols, :])
             proj = pool.tile([P, blocks, OUT], F32, name="proj", tag=tag)
             for s in range(blocks):
@@ -291,13 +291,13 @@ def tile_perception_pb_t_kernel(tc, msg, adj, b2, W3, out):
             run(bias_relu, k - 1)
             run_groups(inverse_root, k)
             run(new_half_a, k + 1)
-            engines = ROW_ENGINES if k > 2 else "GGGV"
+            shares = SHARES if k > 2 else HEAD_SHARES
             if k + 1 < GRAPHS:
-                scale_rows(k + 1, "G", engines)
-                scale_rows(k + 1, "S", engines)
+                scale_rows(k + 1, "G", shares)
+                scale_rows(k + 1, "S", shares)
             run(project, k - 3)
             if k + 1 < GRAPHS:
-                scale_rows(k + 1, "V", engines)
+                scale_rows(k + 1, "V", shares)
             run(quantise_msg, k)
             run(quantise_a, k)
             run(aggregate, k)
@@ -321,7 +321,7 @@ def tile_perception_pb_t_kernel(tc, msg, adj, b2, W3, out):
         sum_degrees(1)
         new_half_a(0)
         for engine in "GVS":
-            scale_rows(0, engine, "VVVS")
+            scale_rows(0, engine, EARLY_SHARES)
         spread_d(0)
         b2_cols = psum_out.tile([P, PACK, OUT], F32, tag="proj", name="b2_cols")
         nc.tensor.transpose(b2_cols[:, 0, :], b2_rows_f32[:], ident[:])
@@ -329,8 +329,9 @@ def tile_perception_pb_t_kernel(tc, msg, adj, b2, W3, out):
         mask_d((1,))
         scale_columns(0)
         new_half_a(1)
-        scale_rows(1, "G", "GGGG")
+        scale_rows(1, "G", SECOND_SHARES)
         regroup_msg(0)
+        scale_rows(1, "S", SECOND_SHARES)
         sum_degrees(2)
         bias = const.tile([P, PACK], F32)
         nc.vector.tensor_copy(out=bias[:], in_=b2_cols[:, 0, 0:PACK])
@@ -367,6 +368,6 @@ def tile_perception_pb_t_kernel(tc, msg, adj, b2, W3, out):
         project(last, 1, 2, psum_h, "sums")
         store(last - 3)
         store(last - 2)
-        store(last - 1)
+        store(last - 1, copy=nc.vector.tensor_copy)
         store(last, 0, 2)
         store(last, 1, 2, nc.vector.tensor_copy)

import concourse.mybir as mybir
from concourse.masks import make_identity

F32 = mybir.dt.float32
BF16 = mybir.dt.bfloat16
U32 = mybir.dt.uint32
U8 = mybir.dt.uint8
FP8X4 = mybir.dt.float8_e4m3fn_x4
ACT = mybir.ActivationFunctionType
ALU = mybir.AluOpType

P = 128
PACK = 4
RUN = 4
GRAPHS = 16
NODES = 512
HIDDEN = 512
OUT = 128
EARLY_SHARES = (("V", 0, 0, 512), ("V", 1, 0, 512), ("V", 2, 0, 512), ("S", 3, 0, 512))
SECOND_SHARES = (("G", 0, 0, 512), ("G", 1, 0, 512), ("G", 2, 0, 512), ("S", 3, 0, 512))
HEAD_SHARES = (("G", 0, 0, 512), ("G", 1, 0, 512), ("G", 2, 0, 512), ("V", 3, 0, 512))
SHARES = (("G", 0, 0, 512), ("G", 1, 0, 512), ("G", 2, 0, 384), ("S", 2, 384, 512), ("V", 3, 0, 512))
ONES_COLS = 48
DEG_GROUPS = ((0,), (1,), (2,), (3,), (4, 5), (6, 7), (8, 9), (10, 11), (12, 13), (14, 15))
WARM_COLS = 512
WARM = 7
DEG_MAX = 2

FLOPS = 2 * GRAPHS * (NODES * NODES * HIDDEN + NODES * HIDDEN * OUT)


def mask_step(group):
    return max(group[-1] - 3, 1)


def by_runs_grouped(grouped):
    return grouped.rearrange("p (c i) t -> p c t i", i=RUN)


def by_runs_rows(planes):
    return planes.rearrange("p t (c i) -> p c t i", i=RUN)


def regroup(copy, grouped, rows):
    copy(out=by_runs_grouped(grouped), in_=by_runs_rows(rows))


def quantise(nc, codes, scales, grouped):
    nc.vector.quantize_mx(
        out=codes.bitcast(FP8X4),
        scales=scales,
        in_=grouped.rearrange("p w t -> p (w t)"),
    )


def tile_perception_pb_t_kernel(tc, msg, adj, b2, W3, out):
    nc = tc.nc
    with (
        tc.tile_pool(name="const", bufs=1) as const,
        tc.tile_pool(name="inputs", bufs=1) as inputs,
        tc.tile_pool(name="work", bufs=2) as work,
        tc.tile_pool(name="ahead", bufs=3) as ahead,
        tc.tile_pool(name="rows", bufs=5) as rows,
        tc.tile_pool(name="results", bufs=5) as results,
        tc.tile_pool(name="h_mx", bufs=4) as h_mx,
        tc.psum_pool(name="psum_deg", bufs=2) as psum_deg,
        tc.psum_pool(name="psum_bcast", bufs=1) as psum_bcast,
        tc.psum_pool(name="psum_h", bufs=PACK) as psum_h,
        tc.psum_pool(name="psum_out", bufs=1) as psum_out,
        tc.manual_schedule(),
    ):
        adj_rows = []
        msg_rows = []

        def load_adj(g):
            adj_g = inputs.tile([P, PACK, NODES], BF16, name="adj%d" % g)
            nc.sync.dma_start(out=adj_g[:], in_=adj[g].rearrange("(t p) i -> p t i", p=P))
            adj_rows.append(adj_g)

        def load_msg(g):
            msg_g = inputs.tile([P, PACK, HIDDEN], BF16, name="msg%d" % g)
            nc.sync.dma_start(out=msg_g[:], in_=msg[g].rearrange("(t p) f -> p t f", p=P))
            msg_rows.append(msg_g)

        load_adj(0)
        w3_rows = const.tile([P, PACK, OUT], BF16)
        nc.sync.dma_start(out=w3_rows[:], in_=W3.rearrange("(t p) o -> p t o", p=P))
        b2_rows = const.tile([P, P], BF16)
        nc.vector.memset(b2_rows[:], 0.0)
        nc.sync.dma_start(out=b2_rows[0:PACK, :], in_=b2.rearrange("(t p) -> t p", p=P))
        load_adj(1)
        for g in range(GRAPHS):
            load_msg(g)
            if g + 2 < GRAPHS:
                load_adj(g + 2)

        ones = const.tile([P, ONES_COLS], BF16)
        nc.vector.memset(ones[:], 1.0)
        blank = const.tile([P, WARM_COLS], BF16)
        nc.gpsimd.memset(blank[:], 0.0)
        floor = const.tile([P, 1], F32)
        nc.vector.memset(floor[:], 1e-30)
        ident = const.tile([P, P], F32)
        make_identity(nc, ident[:])
        for n in range(WARM):
            idle = psum_h.tile([P, WARM_COLS], F32, name="idle", tag="sums")
            nc.tensor.matmul(out=idle[:], lhsT=blank[:, 0:P], rhs=blank[:], start=True, stop=True)

        tiles = {}

        def sum_degrees(g):
            for group in DEG_GROUPS:
                if g == group[0]:
                    tiles["deg", group] = psum_deg.tile([P, DEG_MAX, PACK, ONES_COLS], F32, name="deg")
                if g in group:
                    deg = tiles["deg", group]
                    n = group.index(g)
            for s in range(PACK):
                for t in range(PACK):
                    nc.tensor.matmul(
                        out=deg[:, n, s, :],
                        lhsT=adj_rows[g][:, t, s * P : (s + 1) * P],
                        rhs=ones[:],
                        start=(t == 0),
                        stop=(t == PACK - 1),
                    )

        def inverse_root(group):
            root = work.tile([P, DEG_MAX, PACK], F32, name="root")
            nc.scalar.activation(
                out=root[:, 0 : len(group), :],
                in_=tiles["deg", group][:, 0 : len(group), :, 0],
                func=ACT.Abs_reciprocal_sqrt,
                bias=floor[:],
                scale=1.0,
            )
            tiles["root", group] = root

        def mask_d(group):
            d = work.tile([P, DEG_MAX, PACK], F32, name="d")
            nc.vector.scalar_tensor_tensor(
                out=d[:, 0 : len(group), :],
                in0=tiles["deg", group][:, 0 : len(group), :, 0],
                scalar=0.0,
                in1=tiles["root", group][:, 0 : len(group), :],
                op0=ALU.is_gt,
                op1=ALU.mult,
            )
            for n, g in enumerate(group):
                tiles["d", g] = d[:, n, :]

        def spread_d(g):
            d_all = psum_bcast.tile([P, NODES], F32, name="d_all")
            for t in range(PACK):
                nc.tensor.transpose(
                    d_all[:, t * P : (t + 1) * P],
                    tiles["d", g][:, t : t + 1].to_broadcast([P, P]),
                    ident[:],
                )
            tiles["d_all", g] = d_all

        def new_half_a(g):
            tiles["half_a", g] = rows.tile([P, PACK, NODES], F32, name="half_a", tag="rows")

        def scale_rows(g, engine, shares):
            for name, t, first, end in shares:
                if name != engine:
                    continue
                out = tiles["half_a", g][:, t, first:end]
                in0 = adj_rows[g][:, t, first:end]
                d_t = tiles["d", g][:, t : t + 1]
                if engine == "G":
                    nc.gpsimd.tensor_scalar(
                        out=out, in0=in0, scalar1=d_t, scalar2=0.0, op0=ALU.mult, op1=ALU.add
                    )
                elif engine == "V":
                    nc.vector.tensor_scalar_mul(out=out, in0=in0, scalar1=d_t)
                else:
                    nc.scalar.activation(out=out, in_=in0, func=ACT.Copy, scale=d_t)

        def scale_columns(g):
            a_grouped = work.tile([P, NODES, PACK], BF16, name="a_grouped", align_bytes=64)
            nc.vector.tensor_tensor(
                out=by_runs_grouped(a_grouped[:]),
                in0=by_runs_rows(tiles["half_a", g][:]),
                in1=tiles["d_all", g][:]
                .rearrange("p (c i) -> p c i", i=RUN)
                .unsqueeze(2)
                .to_broadcast([P, NODES // RUN, PACK, RUN]),
                op=ALU.mult,
            )
            tiles["a_grouped", g] = a_grouped

        def regroup_msg(g, copy=nc.scalar.copy):
            msg_grouped = ahead.tile([P, HIDDEN, PACK], BF16, name="msg_grouped", align_bytes=64)
            regroup(copy, msg_grouped[:], msg_rows[g][:])
            tiles["msg_grouped", g] = msg_grouped

        def quantise_msg(g):
            msg_codes = work.tile([P, HIDDEN], U32, name="msg_codes", align_bytes=64)
            msg_scales = work.tile([P, HIDDEN], U8, name="msg_scales", align_bytes=64)
            quantise(nc, msg_codes[:], msg_scales[:], tiles["msg_grouped", g][:])
            tiles["msg_codes", g] = msg_codes
            tiles["msg_scales", g] = msg_scales

        def quantise_a(g):
            a_codes = work.tile([P, NODES], U32, name="a_codes", align_bytes=64)
            a_scales = work.tile([P, NODES], U8, name="a_scales", align_bytes=64)
            quantise(nc, a_codes[:], a_scales[:], tiles["a_grouped", g][:])
            tiles["a_codes", g] = a_codes
            tiles["a_scales", g] = a_scales

        def aggregate(g):
            sums = []
            for t in range(PACK):
                f_cols = slice(t * P, (t + 1) * P)
                sums_t = psum_h.tile([P, NODES], F32, name="sums", tag="sums")
                nc.tensor.matmul_mx(
                    out=sums_t[:],
                    lhsT=tiles["msg_codes", g][:, f_cols].bitcast(FP8X4),
                    lhsT_scale=tiles["msg_scales", g][:, f_cols],
                    rhs=tiles["a_codes", g][:].bitcast(FP8X4),
                    rhs_scale=tiles["a_scales", g][:],
                    start=True,
                    stop=True,
                )
                sums.append(sums_t)
            tiles["sums", g] = sums

        def bias_relu(g):
            h_rows = rows.tile([P, PACK, NODES], BF16, name="h_rows", tag="rows")
            for t in range(PACK):
                nc.scalar.activation(
                    out=h_rows[:, t, :],
                    in_=tiles["sums", g][t][:],
                    func=ACT.Relu,
                    bias=bias[:, t : t + 1],
                    scale=1.0,
                )
            tiles["h_rows", g] = h_rows

        def regroup_h(g, copy=nc.vector.tensor_copy, cols=slice(0, NODES)):
            if ("h_grouped", g) not in tiles:
                tiles["h_grouped", g] = work.tile(
                    [P, NODES, PACK], BF16, name="h_grouped", align_bytes=64
                )
            regroup(copy, tiles["h_grouped", g][:, cols, :], tiles["h_rows", g][:, :, cols])

        def project(g, part=0, parts=1, pool=psum_out, tag="proj"):
            blocks = PACK // parts
            first = part * blocks
            cols = slice(first * P, (first + blocks) * P)
            h_codes = h_mx.tile([P, blocks * P], U32, name="h_codes", align_bytes=64)
            h_scales = h_mx.tile([P, blocks * P], U8, name="h_scales", align_bytes=64)
            quantise(nc, h_codes[:], h_scales[:], tiles["h_grouped", g][:, cols, :])
            proj = pool.tile([P, blocks, OUT], F32, name="proj", tag=tag)
            for s in range(blocks):
                i_cols = slice(s * P, (s + 1) * P)
                nc.tensor.matmul_mx(
                    out=proj[:, s, :],
                    lhsT=h_codes[:, i_cols].bitcast(FP8X4),
                    lhsT_scale=h_scales[:, i_cols],
                    rhs=w3_codes[:].bitcast(FP8X4),
                    rhs_scale=w3_scales[:],
                    start=True,
                    stop=True,
                )
            tiles["proj", g, part] = proj

        def store(g, part=0, parts=1, copy=nc.scalar.copy):
            blocks = PACK // parts
            nodes = slice(part * blocks * P, (part + 1) * blocks * P)
            result = results.tile([P, blocks, OUT], F32, name="result")
            copy(out=result[:], in_=tiles["proj", g, part][:])
            nc.sync.dma_start(out=out[g, nodes].rearrange("(s p) o -> p s o", p=P), in_=result[:])

        def run(stage, g):
            if 0 <= g < GRAPHS:
                stage(g)

        def run_groups(stage, k):
            for group in DEG_GROUPS:
                if len(group) > 1 or group == (3,):
                    if mask_step(group) == k:
                        stage(group)

        def step(k):
            run(scale_columns, k)
            run(spread_d, k + 1)
            run(sum_degrees, k + 4 if k > 1 else k + 3)
            run(bias_relu, k - 1)
            run_groups(inverse_root, k)
            run(new_half_a, k + 1)
            shares = SHARES if k > 2 else HEAD_SHARES
            if k + 1 < GRAPHS:
                scale_rows(k + 1, "G", shares)
                scale_rows(k + 1, "S", shares)
            run(project, k - 3)
            if k + 1 < GRAPHS:
                scale_rows(k + 1, "V", shares)
            run(quantise_msg, k)
            run(quantise_a, k)
            run(aggregate, k)
            if k == 1:
                sum_degrees(k + 4)
            run(regroup_msg, k + 1)
            run(store, k - 3)
            run(regroup_h, k - 2)
            run_groups(mask_d, k)

        sum_degrees(0)
        inverse_root((0,))
        w3_grouped = const.tile([P, OUT, PACK], BF16, align_bytes=64)
        regroup(nc.vector.tensor_copy, w3_grouped[:], w3_rows[:])
        b2_rows_f32 = const.tile([P, P], F32)
        nc.vector.tensor_copy(out=b2_rows_f32[:], in_=b2_rows[:])
        w3_codes = const.tile([P, OUT], U32, align_bytes=64)
        w3_scales = const.tile([P, OUT], U8, align_bytes=64)
        quantise(nc, w3_codes[:], w3_scales[:], w3_grouped[:])
        mask_d((0,))
        sum_degrees(1)
        new_half_a(0)
        for engine in "GVS":
            scale_rows(0, engine, EARLY_SHARES)
        spread_d(0)
        b2_cols = psum_out.tile([P, PACK, OUT], F32, tag="proj", name="b2_cols")
        nc.tensor.transpose(b2_cols[:, 0, :], b2_rows_f32[:], ident[:])
        inverse_root((1,))
        mask_d((1,))
        scale_columns(0)
        new_half_a(1)
        scale_rows(1, "G", SECOND_SHARES)
        regroup_msg(0)
        scale_rows(1, "S", SECOND_SHARES)
        sum_degrees(2)
        bias = const.tile([P, PACK], F32)
        nc.vector.tensor_copy(out=bias[:], in_=b2_cols[:, 0, 0:PACK])
        quantise_msg(0)
        quantise_a(0)
        spread_d(1)
        aggregate(0)
        inverse_root((2,))
        mask_d((2,))
        regroup_msg(1)
        sum_degrees(3)

        for k in range(1, GRAPHS - 1):
            step(k)

        last = GRAPHS - 1
        vector_cols = slice(0, 320)
        scalar_cols = slice(320, NODES)
        scale_columns(last)
        bias_relu(last - 1)
        quantise_msg(last)
        quantise_a(last)
        aggregate(last)
        project(last - 3)
        regroup_h(last - 1, nc.scalar.copy, scalar_cols)
        regroup_h(last - 2)
        regroup_h(last - 1, nc.vector.tensor_copy, vector_cols)
        bias_relu(last)
        project(last - 2, pool=psum_deg, tag="deg")
        regroup_h(last, nc.vector.tensor_copy, vector_cols)
        regroup_h(last, nc.scalar.copy, scalar_cols)
        project(last - 1, pool=psum_deg, tag="deg")
        project(last, 0, 2, psum_h, "sums")
        project(last, 1, 2, psum_h, "sums")
        store(last - 3)
        store(last - 2)
        store(last - 1, copy=nc.vector.tensor_copy)
        store(last, 0, 2)
        store(last, 1, 2, nc.vector.tensor_copy)
